import numpy as np
import ml_dtypes


def mxq(x, axis, fmt="e4m3"):
    dtype, down = {"e4m3": (ml_dtypes.float8_e4m3fn, 7), "e5m2": (ml_dtypes.float8_e5m2, 14)}[fmt]
    v = np.moveaxis(np.asarray(x, np.float32).astype(ml_dtypes.bfloat16).astype(np.float64), axis, -1)
    blocks = v.reshape(v.shape[:-1] + (-1, 32))
    amax = np.abs(blocks).max(-1, keepdims=True)
    byte = np.maximum(np.where(amax > 0, np.frexp(amax)[1] - 1 + 127, 0) - down, 1)
    scale = np.exp2(byte - 127.0)
    codes = (blocks / scale).astype(np.float32).astype(dtype).astype(np.float64)
    return np.moveaxis((codes * scale).reshape(v.shape), -1, axis)


WIDE = False


def mx_kscale(k):
    if not WIDE:
        return np.ones(k)
    levels = np.array([30, -30])
    if k % 512:
        return np.exp2(np.random.permutation(np.resize(levels, k // 32))).repeat(32)
    a = np.empty((k // 512, 16))
    for p in range(k // 512):
        a[p, :8] = np.random.permutation(np.resize(levels, 8))
        for g in range(8):
            far = levels[np.abs(levels - a[p, g]) >= 10]
            a[p, g + 8] = far[np.random.randint(len(far))]
    return np.exp2(a.ravel()).repeat(32)


BF16 = ml_dtypes.bfloat16


def bf(x):
    return np.asarray(x, np.float32).astype(BF16)


def f64(x):
    return np.asarray(x).astype(np.float64)


B, S, D, H, KV, HD = 1, 512, 2048, 16, 4, 128
THETA = 10000.0
HALF = HD // 2


def rope_tables():
    inv_freq = 1.0 / (THETA ** (f64(np.arange(0, HD, 2)) / HD))
    ang = f64(np.arange(S))[:, None] * inv_freq[None, :]
    emb = np.concatenate([ang, ang], axis=-1)
    return np.cos(emb), np.sin(emb)


def rotate_half(t):
    return np.concatenate([-t[..., HALF:], t[..., :HALF]], axis=-1)


def apply_rope(t, cos, sin):
    return t * cos[None, None] + rotate_half(t) * sin[None, None]


def setup_inputs():
    s = mx_kscale(D)
    w = 1.0 / np.sqrt(D)
    return {"x": bf(np.random.standard_normal((B, S, D)) * s),
            "wq": bf(np.random.standard_normal((H * HD, D)) * w / s[None, :]),
            "wk": bf(np.random.standard_normal((KV * HD, D)) * w / s[None, :]),
            "wv": bf(np.random.standard_normal((KV * HD, D)) * w / s[None, :])}


def reference(x, wq, wk, wv):
    xq = mxq(f64(x), 2, "e5m2")
    q = (xq @ mxq(f64(wq), 1, "e5m2").T).reshape(B, S, H, HD).transpose(0, 2, 1, 3)
    k = (xq @ mxq(f64(wk), 1, "e5m2").T).reshape(B, S, KV, HD).transpose(0, 2, 1, 3)
    v = (xq @ mxq(f64(wv), 1, "e5m2").T).reshape(B, S, KV, HD).transpose(0, 2, 1, 3)
    cos, sin = rope_tables()
    return apply_rope(q, cos, sin), apply_rope(k, cos, sin), v

@@ -1,0 +1,236 @@
+from contextlib import ExitStack
+
+import concourse.mybir as mybir
+from concourse.masks import make_identity
+
+F32 = mybir.dt.float32
+BF16 = mybir.dt.bfloat16
+I32 = mybir.dt.int32
+U32 = mybir.dt.uint32
+U8 = mybir.dt.uint8
+E5X4 = mybir.dt.float8_e5m2_x4
+ALU = mybir.AluOpType
+ACT = mybir.ActivationFunctionType
+
+FLOPS = 2 * 512 * 2048 * 3072
+
+P = 128
+HALF = 64
+THETA = 10000.0
+TWO_PI = 6.283185307179586
+N_GROUPS = 7
+FINE_GROUPS = 3
+SHARED_COPY_UNITS = 5
+ADD_ON_GPSIMD = (True, True, True, True)
+
+
+def tile_advancedattn_pa_kernel(tc, x, wq, wk, wv, out_0, out_1, out_2):
+    nc = tc.nc
+
+    with ExitStack() as ctx:
+        const = ctx.enter_context(tc.tile_pool(name="const", bufs=1))
+        rawp = ctx.enter_context(tc.tile_pool(name="rawp", bufs=1))
+        gpool = ctx.enter_context(tc.tile_pool(name="gpool", bufs=4))
+        cpool = ctx.enter_context(tc.tile_pool(name="cpool", bufs=6))
+        epool = ctx.enter_context(tc.tile_pool(name="epool", bufs=4))
+        opool = ctx.enter_context(tc.tile_pool(name="opool", bufs=3))
+        vpool = ctx.enter_context(tc.tile_pool(name="vpool", bufs=4))
+        psum = ctx.enter_context(tc.psum_pool(name="psum", bufs=1))
+        ctx.enter_context(tc.manual_schedule())
+
+        raw = {}
+
+        def group_rows(gi):
+            if gi == 0:
+                return None
+            if gi <= 4:
+                return wq[512 * (gi - 1) : 512 * gi, :]
+            if gi == 5:
+                return wk
+            return wv
+
+        def load(gi, a):
+            cols = slice(1024 * a, 1024 * (a + 1))
+            if gi < FINE_GROUPS:
+                for r in range(4):
+                    t = rawp.tile([P, 1024], BF16, name="raw%d_%d_%d" % (gi, a, r), tag="raw%d_%d_%d" % (gi, a, r))
+                    if gi == 0:
+                        src = x[0].rearrange("(p m) k -> m p k", m=4)[r]
+                    else:
+                        src = group_rows(gi)[P * r : P * (r + 1), :]
+                    nc.sync.dma_start(out=t[:], in_=src[:, cols])
+                    raw[(gi, a, r)] = t[:]
+            else:
+                t = rawp.tile([P, 4, 1024], BF16, name="raw%d_%d" % (gi, a), tag="raw%d_%d" % (gi, a))
+                nc.sync.dma_start(out=t[:], in_=group_rows(gi)[:, cols].rearrange("(r p) k -> p r k", p=P))
+                for r in range(4):
+                    raw[(gi, a, r)] = t[:, r, :]
+
+        for gi, a in ((0, 0), (1, 0), (0, 1), (1, 1)):
+            load(gi, a)
+        for gi in range(2, N_GROUPS):
+            load(gi, 0)
+            load(gi, 1)
+
+        ident = const.tile([P, P], F32, name="ident", tag="ident")
+        make_identity(nc, ident[:])
+        pos_i = const.tile([P, 4], I32, name="pos_i", tag="pos_i")
+        nc.gpsimd.iota(pos_i[:], pattern=[[1, 4]], base=0, channel_multiplier=4)
+
+        zero = const.tile([P, 1], F32, name="zero", tag="zero")
+        warm = const.tile([P, 1], F32, name="warm", tag="warm")
+        nc.vector.memset(zero[:], 0.0)
+        nc.scalar.activation(out=warm[:], in_=zero[:], func=ACT.Sin)
+
+        freq = const.tile([P, HALF], F32, name="freq", tag="freq")
+        nc.vector.memset(freq[:, 0:1], 1.0)
+        s = 1
+        while s < HALF:
+            nc.vector.tensor_scalar(
+                out=freq[:, s : 2 * s], in0=freq[:, 0:s], scalar1=THETA ** (-s / float(HALF)), scalar2=None, op0=ALU.mult
+            )
+            s *= 2
+        pos_f = const.tile([P, 4], F32, name="pos_f", tag="pos_f")
+        nc.vector.tensor_copy(out=pos_f[:], in_=pos_i[:])
+        turns = const.tile([P, 4, HALF], F32, name="turns", tag="turns")
+        for m in range(4):
+            nc.vector.tensor_scalar(
+                out=turns[:, m, :], in0=freq[:], scalar1=pos_f[:, m : m + 1], scalar2=1.0 / TWO_PI, op0=ALU.mult, op1=ALU.mult
+            )
+        whole_i = const.tile([P, 4, HALF], I32, name="whole_i", tag="whole_i")
+        whole_f = const.tile([P, 4, HALF], F32, name="whole_f", tag="whole_f")
+        nc.vector.tensor_copy(out=whole_i[:], in_=turns[:])
+        nc.vector.tensor_copy(out=whole_f[:], in_=whole_i[:])
+        arg = const.tile([P, 2, 4, HALF], F32, name="arg", tag="arg")
+        nc.vector.tensor_tensor(out=arg[:, 0], in0=turns[:], in1=whole_f[:], op=ALU.subtract)
+        nc.vector.tensor_scalar(out=arg[:, 1], in0=arg[:, 0], scalar1=0.25, scalar2=None, op0=ALU.add)
+        wrap = const.tile([P, 2, 4, HALF], F32, name="wrap", tag="wrap")
+        nc.vector.scalar_tensor_tensor(
+            out=wrap[:].rearrange("p a m j -> p (a m j)"),
+            in0=arg[:].rearrange("p a m j -> p (a m j)"),
+            scalar=0.5,
+            in1=arg[:].rearrange("p a m j -> p (a m j)"),
+            op0=ALU.is_gt,
+            op1=ALU.subtract,
+        )
+        table = const.tile([P, 4, 2, P], F32, name="table", tag="table")
+
+        def make_tables():
+            nc.scalar.activation(out=table[:, :, 0, 0:HALF], in_=wrap[:, 1], func=ACT.Sin, scale=-TWO_PI)
+            nc.scalar.activation(out=table[:, :, 0, HALF:P], in_=wrap[:, 1], func=ACT.Sin, scale=-TWO_PI)
+            nc.scalar.activation(out=table[:, :, 1, 0:HALF], in_=wrap[:, 0], func=ACT.Sin, scale=-TWO_PI)
+            nc.scalar.activation(out=table[:, :, 1, HALF:P], in_=wrap[:, 0], func=ACT.Sin, scale=TWO_PI)
+
+        codes = {}
+        scales = {}
+        acc = {}
+        counters = {"t_units": 0}
+
+        def transpose_unit(gi, a):
+            shared = counters["t_units"] < SHARED_COPY_UNITS
+            counters["t_units"] += 1
+            grouped = []
+            for gl in range(2):
+                gq = gpool.tile([P, 2048], BF16, name="gq", tag="gq", align_bytes=64)
+                grouped.append(gq)
+            for rp in range(2):
+                for gl in range(2):
+                    bank = 2 * rp + gl
+                    tp = psum.tile([P, 2, 256], F32, name="tp%d" % bank, tag="tp%d" % bank)
+                    for r2 in range(2):
+                        words = raw[(gi, a, 2 * rp + r2)].bitcast(F32)
+                        for u in range(2):
+                            nc.tensor.transpose(
+                                tp[:, u, P * r2 : P * (r2 + 1)],
+                                words[:, 256 * gl + u : 256 * (gl + 1) : 2],
+                                ident[:],
+                            )
+                    dst = grouped[gl][:].bitcast(F32)[:, 512 * rp : 512 * (rp + 1)].rearrange("p (r u) -> p r u", u=2)
+                    src = tp[:].rearrange("p u r -> p r u")
+                    if shared and bank % 2 == 1:
+                        nc.vector.tensor_copy(out=dst, in_=src)
+                    else:
+                        nc.scalar.copy(out=dst, in_=src)
+            for gl in range(2):
+                g = 2 * a + gl
+                if gi == 0:
+                    cd = const.tile([P, 512], U32, name="xc%d" % g, tag="xc%d" % g, align_bytes=64)
+                    sc = const.tile([P, 512], U8, name="xs%d" % g, tag="xs%d" % g, align_bytes=64)
+                else:
+                    cd = cpool.tile([P, 512], U32, name="wc", tag="wc", align_bytes=64)
+                    sc = cpool.tile([P, 512], U8, name="ws", tag="ws", align_bytes=64)
+                nc.vector.quantize_mx(out=cd[:].bitcast(E5X4), scales=sc[:], in_=grouped[gl][:])
+                codes[(gi, g)] = cd
+                scales[(gi, g)] = sc
+
+        def matmul_unit(gi, a):
+            for m in range(4):
+                if a == 0:
+                    acc[m] = psum.tile([P, 512], F32, name="acc%d" % m, tag="acc%d" % m)
+                for gl in range(2):
+                    g = 2 * a + gl
+                    tok = slice(P * m, P * (m + 1))
+                    nc.tensor.matmul_mx(
+                        out=acc[m][:],
+                        lhsT=codes[(0, g)][:, tok].bitcast(E5X4),
+                        lhsT_scale=scales[(0, g)][:, tok],
+                        rhs=codes[(gi, g)][:].bitcast(E5X4),
+                        rhs_scale=scales[(gi, g)][:],
+                        start=(g == 0),
+                        stop=(g == 3),
+                    )
+
+        def rope_epilogue(gi):
+            ot = opool.tile([P, 4, 4, P], F32, name="ot", tag="ot")
+            for m in range(4):
+                accv = acc[m][:].rearrange("p (h d) -> p h d", h=4)
+                pr = epool.tile([P, 2, 4, P], F32, name="pr", tag="pr")
+                nc.vector.tensor_tensor(
+                    out=pr[:],
+                    in0=accv.unsqueeze(1).to_broadcast([P, 2, 4, P]),
+                    in1=table[:, m].unsqueeze(2).to_broadcast([P, 2, 4, P]),
+                    op=ALU.mult,
+                )
+                eng = nc.gpsimd if ADD_ON_GPSIMD[m] else nc.vector
+                eng.tensor_tensor(out=ot[:, :, m, 0:HALF], in0=pr[:, 0, :, 0:HALF], in1=pr[:, 1, :, HALF:P], op=ALU.add)
+                eng.tensor_tensor(out=ot[:, :, m, HALF:P], in0=pr[:, 0, :, HALF:P], in1=pr[:, 1, :, 0:HALF], op=ALU.add)
+            if gi <= 4:
+                dst = out_0[0, 4 * (gi - 1) : 4 * gi]
+            else:
+                dst = out_1[0]
+            nc.sync.dma_start(
+                out=dst.rearrange("h (p m) d -> p h (m d)", m=4), in_=ot[:].rearrange("p h m d -> p h (m d)")
+            )
+
+        def plain_epilogue():
+            for m in range(4):
+                vt = vpool.tile([P, 4, P], F32, name="vt", tag="vt")
+                accv = acc[m][:].rearrange("p (h d) -> p h d", h=4)
+                if m % 2 == 0:
+                    nc.scalar.copy(out=vt[:], in_=accv)
+                else:
+                    nc.vector.tensor_copy(out=vt[:], in_=accv)
+                nc.sync.dma_start(out=out_2[0].rearrange("h (p m) d -> m p h d", m=4)[m], in_=vt[:])
+
+        def finish(gi):
+            if gi < 6:
+                rope_epilogue(gi)
+            else:
+                plain_epilogue()
+
+        transpose_unit(0, 0)
+        transpose_unit(1, 0)
+        transpose_unit(0, 1)
+        make_tables()
+        matmul_unit(1, 0)
+        transpose_unit(1, 1)
+        transpose_unit(2, 0)
+        matmul_unit(1, 1)
+        finish(1)
+        for gi in range(2, N_GROUPS):
+            transpose_unit(gi, 1)
+            matmul_unit(gi, 0)
+            if gi + 1 < N_GROUPS:
+                transpose_unit(gi + 1, 0)
+            matmul_unit(gi, 1)
+            finish(gi)

@@ -22,6 +22,9 @@ N_GROUPS = 7
 FINE_GROUPS = 3
 SHARED_COPY_UNITS = 5
 ADD_ON_GPSIMD = (True, True, True, True)
+PREWARM = 6
+WARM_UNITS = 5
+FULL_WARM_UNITS = 3
 
 
 def tile_advancedattn_pa_kernel(tc, x, wq, wk, wv, out_0, out_1, out_2):
@@ -77,6 +80,8 @@ def tile_advancedattn_pa_kernel(tc, x, wq, wk, wv, out_0, out_1, out_2):
         pos_i = const.tile([P, 4], I32, name="pos_i", tag="pos_i")
         nc.gpsimd.iota(pos_i[:], pattern=[[1, 4]], base=0, channel_multiplier=4)
 
+        ones = const.tile([P, 512], BF16, name="ones", tag="ones")
+        nc.vector.memset(ones[:], 1.0)
         zero = const.tile([P, 1], F32, name="zero", tag="zero")
         warm = const.tile([P, 1], F32, name="warm", tag="warm")
         nc.vector.memset(zero[:], 0.0)
@@ -127,7 +132,8 @@ def tile_advancedattn_pa_kernel(tc, x, wq, wk, wv, out_0, out_1, out_2):
         counters = {"t_units": 0}
 
         def transpose_unit(gi, a):
-            shared = counters["t_units"] < SHARED_COPY_UNITS
+            unit = counters["t_units"]
+            shared = unit < SHARED_COPY_UNITS
             counters["t_units"] += 1
             grouped = []
             for gl in range(2):
@@ -137,6 +143,15 @@ def tile_advancedattn_pa_kernel(tc, x, wq, wk, wv, out_0, out_1, out_2):
                 for gl in range(2):
                     bank = 2 * rp + gl
                     tp = psum.tile([P, 2, 256], F32, name="tp%d" % bank, tag="tp%d" % bank)
+                    n_dummy = 0
+                    if unit < FULL_WARM_UNITS or (unit < WARM_UNITS and bank % 2 == 0):
+                        n_dummy = 1
+                    if unit == 0 and bank == 0:
+                        n_dummy = PREWARM
+                    for i in range(n_dummy):
+                        nc.tensor.matmul(
+                            out=tp[:].rearrange("p u r -> p (u r)"), lhsT=ones[:, 0:P], rhs=ones[:], start=True, stop=True
+                        )
                     for r2 in range(2):
                         words = raw[(gi, a, 2 * rp + r2)].bitcast(F32)
                         for u in range(2):

@@ -21,10 +21,10 @@ TWO_PI = 6.283185307179586
 N_GROUPS = 7
 FINE_GROUPS = 3
 SHARED_COPY_UNITS = 5
-ADD_ON_GPSIMD = (True, True, True, True)
-PREWARM = 6
-WARM_UNITS = 5
-FULL_WARM_UNITS = 3
+ADD_ON_GPSIMD = (True, True, False, False)
+ROW_MAJOR_UNITS = 5
+SORT_FROM_GROUP = 3
+SORTED_ROW_TILES = 3
 
 
 def tile_advancedattn_pa_kernel(tc, x, wq, wk, wv, out_0, out_1, out_2):
@@ -38,6 +38,7 @@ def tile_advancedattn_pa_kernel(tc, x, wq, wk, wv, out_0, out_1, out_2):
         epool = ctx.enter_context(tc.tile_pool(name="epool", bufs=4))
         opool = ctx.enter_context(tc.tile_pool(name="opool", bufs=3))
         vpool = ctx.enter_context(tc.tile_pool(name="vpool", bufs=4))
+        dpool = ctx.enter_context(tc.tile_pool(name="dpool", bufs=6))
         psum = ctx.enter_context(tc.psum_pool(name="psum", bufs=1))
         ctx.enter_context(tc.manual_schedule())
 
@@ -80,8 +81,6 @@ def tile_advancedattn_pa_kernel(tc, x, wq, wk, wv, out_0, out_1, out_2):
         pos_i = const.tile([P, 4], I32, name="pos_i", tag="pos_i")
         nc.gpsimd.iota(pos_i[:], pattern=[[1, 4]], base=0, channel_multiplier=4)
 
-        ones = const.tile([P, 512], BF16, name="ones", tag="ones")
-        nc.vector.memset(ones[:], 1.0)
         zero = const.tile([P, 1], F32, name="zero", tag="zero")
         warm = const.tile([P, 1], F32, name="warm", tag="warm")
         nc.vector.memset(zero[:], 0.0)
@@ -130,42 +129,45 @@ def tile_advancedattn_pa_kernel(tc, x, wq, wk, wv, out_0, out_1, out_2):
         scales = {}
         acc = {}
         counters = {"t_units": 0}
+        sorted_words = {}
+        late = []
+
+        def sort_unit(gi, a):
+            if gi < SORT_FROM_GROUP:
+                return
+            for r in range(SORTED_ROW_TILES):
+                dt = dpool.tile([P, 2, 2, P], F32, name="dt", tag="dt")
+                nc.scalar.copy(out=dt[:], in_=raw[(gi, a, r)].bitcast(F32).rearrange("p (g w u) -> p g u w", g=2, u=2))
+                sorted_words[(gi, a, r)] = dt
 
         def transpose_unit(gi, a):
             unit = counters["t_units"]
             shared = unit < SHARED_COPY_UNITS
+            if unit < ROW_MAJOR_UNITS:
+                banks = ((0, 0), (0, 1), (1, 0), (1, 1))
+            else:
+                banks = ((0, 0), (1, 0), (0, 1), (1, 1))
             counters["t_units"] += 1
             grouped = []
             for gl in range(2):
                 gq = gpool.tile([P, 2048], BF16, name="gq", tag="gq", align_bytes=64)
                 grouped.append(gq)
-            for rp in range(2):
-                for gl in range(2):
-                    bank = 2 * rp + gl
-                    tp = psum.tile([P, 2, 256], F32, name="tp%d" % bank, tag="tp%d" % bank)
-                    n_dummy = 0
-                    if unit < FULL_WARM_UNITS or (unit < WARM_UNITS and bank % 2 == 0):
-                        n_dummy = 1
-                    if unit == 0 and bank == 0:
-                        n_dummy = PREWARM
-                    for i in range(n_dummy):
-                        nc.tensor.matmul(
-                            out=tp[:].rearrange("p u r -> p (u r)"), lhsT=ones[:, 0:P], rhs=ones[:], start=True, stop=True
-                        )
-                    for r2 in range(2):
-                        words = raw[(gi, a, 2 * rp + r2)].bitcast(F32)
-                        for u in range(2):
-                            nc.tensor.transpose(
-                                tp[:, u, P * r2 : P * (r2 + 1)],
-                                words[:, 256 * gl + u : 256 * (gl + 1) : 2],
-                                ident[:],
-                            )
-                    dst = grouped[gl][:].bitcast(F32)[:, 512 * rp : 512 * (rp + 1)].rearrange("p (r u) -> p r u", u=2)
-                    src = tp[:].rearrange("p u r -> p r u")
-                    if shared and bank % 2 == 1:
-                        nc.vector.tensor_copy(out=dst, in_=src)
-                    else:
-                        nc.scalar.copy(out=dst, in_=src)
+            for bank, (rp, gl) in enumerate(banks):
+                tp = psum.tile([P, 2, 256], F32, name="tp%d" % bank, tag="tp%d" % bank)
+                for r2 in range(2):
+                    key = (gi, a, 2 * rp + r2)
+                    for u in range(2):
+                        if key in sorted_words:
+                            words = sorted_words[key][:, gl, u, :]
+                        else:
+                            words = raw[key].bitcast(F32)[:, 256 * gl + u : 256 * (gl + 1) : 2]
+                        nc.tensor.transpose(tp[:, u, P * r2 : P * (r2 + 1)], words, ident[:])
+                dst = grouped[gl][:].bitcast(F32)[:, 512 * rp : 512 * (rp + 1)].rearrange("p (r u) -> p r u", u=2)
+                src = tp[:].rearrange("p u r -> p r u")
+                if shared and bank % 2 == 1:
+                    nc.vector.tensor_copy(out=dst, in_=src)
+                else:
+                    nc.scalar.copy(out=dst, in_=src)
             for gl in range(2):
                 g = 2 * a + gl
                 if gi == 0:
@@ -177,6 +179,7 @@ def tile_advancedattn_pa_kernel(tc, x, wq, wk, wv, out_0, out_1, out_2):
                 nc.vector.quantize_mx(out=cd[:].bitcast(E5X4), scales=sc[:], in_=grouped[gl][:])
                 codes[(gi, g)] = cd
                 scales[(gi, g)] = sc
+            flush_late()
 
         def matmul_unit(gi, a):
             for m in range(4):
@@ -195,6 +198,24 @@ def tile_advancedattn_pa_kernel(tc, x, wq, wk, wv, out_0, out_1, out_2):
                         stop=(g == 3),
                     )
 
+        def rope_add(eng, ot, pr, m):
+            eng.tensor_tensor(out=ot[:, :, m, 0:HALF], in0=pr[:, 0, :, 0:HALF], in1=pr[:, 1, :, HALF:P], op=ALU.add)
+            eng.tensor_tensor(out=ot[:, :, m, HALF:P], in0=pr[:, 0, :, HALF:P], in1=pr[:, 1, :, 0:HALF], op=ALU.add)
+
+        def flush_late():
+            for ot, pr, m in late:
+                if pr is not None:
+                    rope_add(nc.vector, ot, pr, m)
+                    continue
+                if m <= 4:
+                    dst = out_0[0, 4 * (m - 1) : 4 * m]
+                else:
+                    dst = out_1[0]
+                nc.sync.dma_start(
+                    out=dst.rearrange("h (p m) d -> p h (m d)", m=4), in_=ot[:].rearrange("p h m d -> p h (m d)")
+                )
+            late.clear()
+
         def rope_epilogue(gi):
             ot = opool.tile([P, 4, 4, P], F32, name="ot", tag="ot")
             for m in range(4):
@@ -202,20 +223,15 @@ def tile_advancedattn_pa_kernel(tc, x, wq, wk, wv, out_0, out_1, out_2):
                 pr = epool.tile([P, 2, 4, P], F32, name="pr", tag="pr")
                 nc.vector.tensor_tensor(
                     out=pr[:],
-                    in0=accv.unsqueeze(1).to_broadcast([P, 2, 4, P]),
-                    in1=table[:, m].unsqueeze(2).to_broadcast([P, 2, 4, P]),
+                    in0=table[:, m].unsqueeze(2).to_broadcast([P, 2, 4, P]),
+                    in1=accv.unsqueeze(1).to_broadcast([P, 2, 4, P]),
                     op=ALU.mult,
                 )
-                eng = nc.gpsimd if ADD_ON_GPSIMD[m] else nc.vector
-                eng.tensor_tensor(out=ot[:, :, m, 0:HALF], in0=pr[:, 0, :, 0:HALF], in1=pr[:, 1, :, HALF:P], op=ALU.add)
-                eng.tensor_tensor(out=ot[:, :, m, HALF:P], in0=pr[:, 0, :, HALF:P], in1=pr[:, 1, :, 0:HALF], op=ALU.add)
-            if gi <= 4:
-                dst = out_0[0, 4 * (gi - 1) : 4 * gi]
-            else:
-                dst = out_1[0]
-            nc.sync.dma_start(
-                out=dst.rearrange("h (p m) d -> p h (m d)", m=4), in_=ot[:].rearrange("p h m d -> p h (m d)")
-            )
+                if ADD_ON_GPSIMD[m]:
+                    rope_add(nc.gpsimd, ot, pr, m)
+                else:
+                    late.append((ot, pr, m))
+            late.append((ot, None, gi))
 
         def plain_epilogue():
             for m in range(4):
@@ -244,8 +260,11 @@ def tile_advancedattn_pa_kernel(tc, x, wq, wk, wv, out_0, out_1, out_2):
         finish(1)
         for gi in range(2, N_GROUPS):
             transpose_unit(gi, 1)
+            if gi + 1 < N_GROUPS:
+                sort_unit(gi + 1, 0)
             matmul_unit(gi, 0)
             if gi + 1 < N_GROUPS:
                 transpose_unit(gi + 1, 0)
+                sort_unit(gi + 1, 1)
             matmul_unit(gi, 1)
             finish(gi)

@@ -20,11 +20,12 @@ THETA = 10000.0
 TWO_PI = 6.283185307179586
 N_GROUPS = 7
 FINE_GROUPS = 3
-SHARED_COPY_UNITS = 5
+SHARED_COPY_UNITS = 3
+VECTOR_COPY_UNIT = 3
 ADD_ON_GPSIMD = (True, True, False, False)
 ROW_MAJOR_UNITS = 5
-SORT_FROM_GROUP = 3
-SORTED_ROW_TILES = 3
+STEADY_GROUP = 3
+SORTED_ROW_TILES = (3, 4)
 
 
 def tile_advancedattn_pa_kernel(tc, x, wq, wk, wv, out_0, out_1, out_2):
@@ -38,7 +39,7 @@ def tile_advancedattn_pa_kernel(tc, x, wq, wk, wv, out_0, out_1, out_2):
         epool = ctx.enter_context(tc.tile_pool(name="epool", bufs=4))
         opool = ctx.enter_context(tc.tile_pool(name="opool", bufs=3))
         vpool = ctx.enter_context(tc.tile_pool(name="vpool", bufs=4))
-        dpool = ctx.enter_context(tc.tile_pool(name="dpool", bufs=6))
+        dpool = ctx.enter_context(tc.tile_pool(name="dpool", bufs=8))
         psum = ctx.enter_context(tc.psum_pool(name="psum", bufs=1))
         ctx.enter_context(tc.manual_schedule())
 
@@ -119,9 +120,11 @@ def tile_advancedattn_pa_kernel(tc, x, wq, wk, wv, out_0, out_1, out_2):
         )
         table = const.tile([P, 4, 2, P], F32, name="table", tag="table")
 
-        def make_tables():
+        def make_cos_table():
             nc.scalar.activation(out=table[:, :, 0, 0:HALF], in_=wrap[:, 1], func=ACT.Sin, scale=-TWO_PI)
             nc.scalar.activation(out=table[:, :, 0, HALF:P], in_=wrap[:, 1], func=ACT.Sin, scale=-TWO_PI)
+
+        def make_sin_table():
             nc.scalar.activation(out=table[:, :, 1, 0:HALF], in_=wrap[:, 0], func=ACT.Sin, scale=-TWO_PI)
             nc.scalar.activation(out=table[:, :, 1, HALF:P], in_=wrap[:, 0], func=ACT.Sin, scale=TWO_PI)
 
@@ -133,9 +136,8 @@ def tile_advancedattn_pa_kernel(tc, x, wq, wk, wv, out_0, out_1, out_2):
         late = []
 
         def sort_unit(gi, a):
-            if gi < SORT_FROM_GROUP:
-                return
-            for r in range(SORTED_ROW_TILES):
+            n_sorted = SORTED_ROW_TILES[a] if gi >= STEADY_GROUP else 4
+            for r in range(n_sorted):
                 dt = dpool.tile([P, 2, 2, P], F32, name="dt", tag="dt")
                 nc.scalar.copy(out=dt[:], in_=raw[(gi, a, r)].bitcast(F32).rearrange("p (g w u) -> p g u w", g=2, u=2))
                 sorted_words[(gi, a, r)] = dt
@@ -164,7 +166,7 @@ def tile_advancedattn_pa_kernel(tc, x, wq, wk, wv, out_0, out_1, out_2):
                         nc.tensor.transpose(tp[:, u, P * r2 : P * (r2 + 1)], words, ident[:])
                 dst = grouped[gl][:].bitcast(F32)[:, 512 * rp : 512 * (rp + 1)].rearrange("p (r u) -> p r u", u=2)
                 src = tp[:].rearrange("p u r -> p r u")
-                if shared and bank % 2 == 1:
+                if (shared and bank % 2 == 1) or unit == VECTOR_COPY_UNIT:
                     nc.vector.tensor_copy(out=dst, in_=src)
                 else:
                     nc.scalar.copy(out=dst, in_=src)
@@ -250,12 +252,16 @@ def tile_advancedattn_pa_kernel(tc, x, wq, wk, wv, out_0, out_1, out_2):
                 plain_epilogue()
 
         transpose_unit(0, 0)
+        make_cos_table()
         transpose_unit(1, 0)
+        make_sin_table()
         transpose_unit(0, 1)
-        make_tables()
+        sort_unit(1, 1)
+        sort_unit(2, 0)
         matmul_unit(1, 0)
         transpose_unit(1, 1)
         transpose_unit(2, 0)
+        sort_unit(2, 1)
         matmul_unit(1, 1)
         finish(1)
         for gi in range(2, N_GROUPS):

@@ -20,12 +20,11 @@ THETA = 10000.0
 TWO_PI = 6.283185307179586
 N_GROUPS = 7
 FINE_GROUPS = 3
-SHARED_COPY_UNITS = 3
-VECTOR_COPY_UNIT = 3
+SHARED_COPY_UNITS = 5
 ADD_ON_GPSIMD = (True, True, False, False)
 ROW_MAJOR_UNITS = 5
-STEADY_GROUP = 3
-SORTED_ROW_TILES = (3, 4)
+SORT_FROM_GROUP = 3
+SORTED_ROW_TILES = 3
 
 
 def tile_advancedattn_pa_kernel(tc, x, wq, wk, wv, out_0, out_1, out_2):
@@ -39,7 +38,7 @@ def tile_advancedattn_pa_kernel(tc, x, wq, wk, wv, out_0, out_1, out_2):
         epool = ctx.enter_context(tc.tile_pool(name="epool", bufs=4))
         opool = ctx.enter_context(tc.tile_pool(name="opool", bufs=3))
         vpool = ctx.enter_context(tc.tile_pool(name="vpool", bufs=4))
-        dpool = ctx.enter_context(tc.tile_pool(name="dpool", bufs=8))
+        dpool = ctx.enter_context(tc.tile_pool(name="dpool", bufs=6))
         psum = ctx.enter_context(tc.psum_pool(name="psum", bufs=1))
         ctx.enter_context(tc.manual_schedule())
 
@@ -120,11 +119,9 @@ def tile_advancedattn_pa_kernel(tc, x, wq, wk, wv, out_0, out_1, out_2):
         )
         table = const.tile([P, 4, 2, P], F32, name="table", tag="table")
 
-        def make_cos_table():
+        def make_tables():
             nc.scalar.activation(out=table[:, :, 0, 0:HALF], in_=wrap[:, 1], func=ACT.Sin, scale=-TWO_PI)
             nc.scalar.activation(out=table[:, :, 0, HALF:P], in_=wrap[:, 1], func=ACT.Sin, scale=-TWO_PI)
-
-        def make_sin_table():
             nc.scalar.activation(out=table[:, :, 1, 0:HALF], in_=wrap[:, 0], func=ACT.Sin, scale=-TWO_PI)
             nc.scalar.activation(out=table[:, :, 1, HALF:P], in_=wrap[:, 0], func=ACT.Sin, scale=TWO_PI)
 
@@ -136,8 +133,9 @@ def tile_advancedattn_pa_kernel(tc, x, wq, wk, wv, out_0, out_1, out_2):
         late = []
 
         def sort_unit(gi, a):
-            n_sorted = SORTED_ROW_TILES[a] if gi >= STEADY_GROUP else 4
-            for r in range(n_sorted):
+            if gi < SORT_FROM_GROUP:
+                return
+            for r in range(SORTED_ROW_TILES):
                 dt = dpool.tile([P, 2, 2, P], F32, name="dt", tag="dt")
                 nc.scalar.copy(out=dt[:], in_=raw[(gi, a, r)].bitcast(F32).rearrange("p (g w u) -> p g u w", g=2, u=2))
                 sorted_words[(gi, a, r)] = dt
@@ -166,7 +164,7 @@ def tile_advancedattn_pa_kernel(tc, x, wq, wk, wv, out_0, out_1, out_2):
                         nc.tensor.transpose(tp[:, u, P * r2 : P * (r2 + 1)], words, ident[:])
                 dst = grouped[gl][:].bitcast(F32)[:, 512 * rp : 512 * (rp + 1)].rearrange("p (r u) -> p r u", u=2)
                 src = tp[:].rearrange("p u r -> p r u")
-                if (shared and bank % 2 == 1) or unit == VECTOR_COPY_UNIT:
+                if shared and bank % 2 == 1:
                     nc.vector.tensor_copy(out=dst, in_=src)
                 else:
                     nc.scalar.copy(out=dst, in_=src)
@@ -204,18 +202,23 @@ def tile_advancedattn_pa_kernel(tc, x, wq, wk, wv, out_0, out_1, out_2):
             eng.tensor_tensor(out=ot[:, :, m, 0:HALF], in0=pr[:, 0, :, 0:HALF], in1=pr[:, 1, :, HALF:P], op=ALU.add)
             eng.tensor_tensor(out=ot[:, :, m, HALF:P], in0=pr[:, 0, :, HALF:P], in1=pr[:, 1, :, 0:HALF], op=ALU.add)
 
+        def store_pair(ot, gi, pair):
+            if gi <= 4:
+                dst = out_0[0, 4 * (gi - 1) : 4 * gi]
+            else:
+                dst = out_1[0]
+            cols = slice(2 * P * pair, 2 * P * (pair + 1))
+            nc.sync.dma_start(
+                out=dst.rearrange("h (p m) d -> p h (m d)", m=4)[:, :, cols],
+                in_=ot[:].rearrange("p h m d -> p h (m d)")[:, :, cols],
+            )
+
         def flush_late():
             for ot, pr, m in late:
                 if pr is not None:
                     rope_add(nc.vector, ot, pr, m)
-                    continue
-                if m <= 4:
-                    dst = out_0[0, 4 * (m - 1) : 4 * m]
                 else:
-                    dst = out_1[0]
-                nc.sync.dma_start(
-                    out=dst.rearrange("h (p m) d -> p h (m d)", m=4), in_=ot[:].rearrange("p h m d -> p h (m d)")
-                )
+                    store_pair(ot, m, 1)
             late.clear()
 
         def rope_epilogue(gi):
@@ -233,6 +236,7 @@ def tile_advancedattn_pa_kernel(tc, x, wq, wk, wv, out_0, out_1, out_2):
                     rope_add(nc.gpsimd, ot, pr, m)
                 else:
                     late.append((ot, pr, m))
+            store_pair(ot, gi, 0)
             late.append((ot, None, gi))
 
         def plain_epilogue():
@@ -252,16 +256,12 @@ def tile_advancedattn_pa_kernel(tc, x, wq, wk, wv, out_0, out_1, out_2):
                 plain_epilogue()
 
         transpose_unit(0, 0)
-        make_cos_table()
         transpose_unit(1, 0)
-        make_sin_table()
         transpose_unit(0, 1)
-        sort_unit(1, 1)
-        sort_unit(2, 0)
+        make_tables()
         matmul_unit(1, 0)
         transpose_unit(1, 1)
         transpose_unit(2, 0)
-        sort_unit(2, 1)
         matmul_unit(1, 1)
         finish(1)
         for gi in range(2, N_GROUPS):

@@ -20,11 +20,10 @@ THETA = 10000.0
 TWO_PI = 6.283185307179586
 N_GROUPS = 7
 FINE_GROUPS = 3
-SHARED_COPY_UNITS = 5
 ADD_ON_GPSIMD = (True, True, False, False)
-ROW_MAJOR_UNITS = 5
 SORT_FROM_GROUP = 3
-SORTED_ROW_TILES = 3
+SORTED_ROW_TILES = (1, 2, 3)
+REUSE_FROM_GROUP = 5
 
 
 def tile_advancedattn_pa_kernel(tc, x, wq, wk, wv, out_0, out_1, out_2):
@@ -33,8 +32,8 @@ def tile_advancedattn_pa_kernel(tc, x, wq, wk, wv, out_0, out_1, out_2):
     with ExitStack() as ctx:
         const = ctx.enter_context(tc.tile_pool(name="const", bufs=1))
         rawp = ctx.enter_context(tc.tile_pool(name="rawp", bufs=1))
-        gpool = ctx.enter_context(tc.tile_pool(name="gpool", bufs=4))
-        cpool = ctx.enter_context(tc.tile_pool(name="cpool", bufs=6))
+        gpool = ctx.enter_context(tc.tile_pool(name="gpool", bufs=3))
+        cpool = ctx.enter_context(tc.tile_pool(name="cpool", bufs=4))
         epool = ctx.enter_context(tc.tile_pool(name="epool", bufs=4))
         opool = ctx.enter_context(tc.tile_pool(name="opool", bufs=3))
         vpool = ctx.enter_context(tc.tile_pool(name="vpool", bufs=4))
@@ -45,8 +44,6 @@ def tile_advancedattn_pa_kernel(tc, x, wq, wk, wv, out_0, out_1, out_2):
         raw = {}
 
         def group_rows(gi):
-            if gi == 0:
-                return None
             if gi <= 4:
                 return wq[512 * (gi - 1) : 512 * gi, :]
             if gi == 5:
@@ -65,14 +62,15 @@ def tile_advancedattn_pa_kernel(tc, x, wq, wk, wv, out_0, out_1, out_2):
                     nc.sync.dma_start(out=t[:], in_=src[:, cols])
                     raw[(gi, a, r)] = t[:]
             else:
-                t = rawp.tile([P, 4, 1024], BF16, name="raw%d_%d" % (gi, a), tag="raw%d_%d" % (gi, a))
+                slot = gi - 2 if gi >= REUSE_FROM_GROUP else gi
+                t = rawp.tile([P, 4, 1024], BF16, name="raw%d_%d" % (gi, a), tag="raw%d_%d" % (slot, a))
                 nc.sync.dma_start(out=t[:], in_=group_rows(gi)[:, cols].rearrange("(r p) k -> p r k", p=P))
                 for r in range(4):
                     raw[(gi, a, r)] = t[:, r, :]
 
         for gi, a in ((0, 0), (1, 0), (0, 1), (1, 1)):
             load(gi, a)
-        for gi in range(2, N_GROUPS):
+        for gi in range(2, REUSE_FROM_GROUP):
             load(gi, 0)
             load(gi, 1)
 
@@ -125,77 +123,63 @@ def tile_advancedattn_pa_kernel(tc, x, wq, wk, wv, out_0, out_1, out_2):
             nc.scalar.activation(out=table[:, :, 1, 0:HALF], in_=wrap[:, 0], func=ACT.Sin, scale=-TWO_PI)
             nc.scalar.activation(out=table[:, :, 1, HALF:P], in_=wrap[:, 0], func=ACT.Sin, scale=TWO_PI)
 
+        grouped = {}
         codes = {}
         scales = {}
         acc = {}
-        counters = {"t_units": 0}
         sorted_words = {}
-        late = []
+        products = {}
+        outputs = {}
 
         def sort_unit(gi, a):
-            if gi < SORT_FROM_GROUP:
-                return
-            for r in range(SORTED_ROW_TILES):
+            for r in SORTED_ROW_TILES:
                 dt = dpool.tile([P, 2, 2, P], F32, name="dt", tag="dt")
                 nc.scalar.copy(out=dt[:], in_=raw[(gi, a, r)].bitcast(F32).rearrange("p (g w u) -> p g u w", g=2, u=2))
                 sorted_words[(gi, a, r)] = dt
 
         def transpose_unit(gi, a):
-            unit = counters["t_units"]
-            shared = unit < SHARED_COPY_UNITS
-            if unit < ROW_MAJOR_UNITS:
-                banks = ((0, 0), (0, 1), (1, 0), (1, 1))
-            else:
-                banks = ((0, 0), (1, 0), (0, 1), (1, 1))
-            counters["t_units"] += 1
-            grouped = []
-            for gl in range(2):
-                gq = gpool.tile([P, 2048], BF16, name="gq", tag="gq", align_bytes=64)
-                grouped.append(gq)
-            for bank, (rp, gl) in enumerate(banks):
-                tp = psum.tile([P, 2, 256], F32, name="tp%d" % bank, tag="tp%d" % bank)
-                for r2 in range(2):
-                    key = (gi, a, 2 * rp + r2)
+            gq = gpool.tile([P, 4096], BF16, name="gq", tag="gq", align_bytes=64)
+            grouped[(gi, a)] = gq
+            gq_words = gq[:].bitcast(F32).rearrange("p (g r c u) -> p g r c u", g=2, r=4, u=2)
+            for r in range(4):
+                tp = psum.tile([P, 2, 2, P], F32, name="tp%d" % r, tag="tp%d" % r)
+                key = (gi, a, r)
+                for gl in range(2):
                     for u in range(2):
                         if key in sorted_words:
                             words = sorted_words[key][:, gl, u, :]
                         else:
                             words = raw[key].bitcast(F32)[:, 256 * gl + u : 256 * (gl + 1) : 2]
-                        nc.tensor.transpose(tp[:, u, P * r2 : P * (r2 + 1)], words, ident[:])
-                dst = grouped[gl][:].bitcast(F32)[:, 512 * rp : 512 * (rp + 1)].rearrange("p (r u) -> p r u", u=2)
-                src = tp[:].rearrange("p u r -> p r u")
-                if shared and bank % 2 == 1:
-                    nc.vector.tensor_copy(out=dst, in_=src)
-                else:
-                    nc.scalar.copy(out=dst, in_=src)
-            for gl in range(2):
-                g = 2 * a + gl
-                if gi == 0:
-                    cd = const.tile([P, 512], U32, name="xc%d" % g, tag="xc%d" % g, align_bytes=64)
-                    sc = const.tile([P, 512], U8, name="xs%d" % g, tag="xs%d" % g, align_bytes=64)
-                else:
-                    cd = cpool.tile([P, 512], U32, name="wc", tag="wc", align_bytes=64)
-                    sc = cpool.tile([P, 512], U8, name="ws", tag="ws", align_bytes=64)
-                nc.vector.quantize_mx(out=cd[:].bitcast(E5X4), scales=sc[:], in_=grouped[gl][:])
-                codes[(gi, g)] = cd
-                scales[(gi, g)] = sc
-            flush_late()
+                        nc.tensor.transpose(tp[:, gl, u, :], words, ident[:])
+                nc.scalar.copy(out=gq_words[:, :, r], in_=tp[:].rearrange("p g u c -> p g c u"))
+
+        def quantize_unit(gi, a):
+            if gi == 0:
+                cd = const.tile([P, 1024], U32, name="xc%d" % a, tag="xc%d" % a, align_bytes=64)
+                sc = const.tile([P, 1024], U8, name="xs%d" % a, tag="xs%d" % a, align_bytes=64)
+            else:
+                cd = cpool.tile([P, 1024], U32, name="wc", tag="wc", align_bytes=64)
+                sc = cpool.tile([P, 1024], U8, name="ws", tag="ws", align_bytes=64)
+            nc.vector.quantize_mx(out=cd[:].bitcast(E5X4), scales=sc[:], in_=grouped[(gi, a)][:])
+            codes[(gi, a)] = cd
+            scales[(gi, a)] = sc
 
         def matmul_unit(gi, a):
+            bank_tag = "tp%d" if gi == N_GROUPS - 1 else "acc%d"
             for m in range(4):
                 if a == 0:
-                    acc[m] = psum.tile([P, 512], F32, name="acc%d" % m, tag="acc%d" % m)
+                    acc[m] = psum.tile([P, 512], F32, name="acc%d" % m, tag=bank_tag % m)
                 for gl in range(2):
-                    g = 2 * a + gl
-                    tok = slice(P * m, P * (m + 1))
+                    tok = slice(512 * gl + P * m, 512 * gl + P * (m + 1))
+                    chan = slice(512 * gl, 512 * (gl + 1))
                     nc.tensor.matmul_mx(
                         out=acc[m][:],
-                        lhsT=codes[(0, g)][:, tok].bitcast(E5X4),
-                        lhsT_scale=scales[(0, g)][:, tok],
-                        rhs=codes[(gi, g)][:].bitcast(E5X4),
-                        rhs_scale=scales[(gi, g)][:],
-                        start=(g == 0),
-                        stop=(g == 3),
+                        lhsT=codes[(0, a)][:, tok].bitcast(E5X4),
+                        lhsT_scale=scales[(0, a)][:, tok],
+                        rhs=codes[(gi, a)][:, chan].bitcast(E5X4),
+                        rhs_scale=scales[(gi, a)][:, chan],
+                        start=(a == 0 and gl == 0),
+                        stop=(a == 1 and gl == 1),
                     )
 
         def rope_add(eng, ot, pr, m):
@@ -213,19 +197,13 @@ def tile_advancedattn_pa_kernel(tc, x, wq, wk, wv, out_0, out_1, out_2):
                 in_=ot[:].rearrange("p h m d -> p h (m d)")[:, :, cols],
             )
 
-        def flush_late():
-            for ot, pr, m in late:
-                if pr is not None:
-                    rope_add(nc.vector, ot, pr, m)
-                else:
-                    store_pair(ot, m, 1)
-            late.clear()
-
-        def rope_epilogue(gi):
+        def rope_products(gi):
             ot = opool.tile([P, 4, 4, P], F32, name="ot", tag="ot")
+            outputs[gi] = ot
             for m in range(4):
                 accv = acc[m][:].rearrange("p (h d) -> p h d", h=4)
                 pr = epool.tile([P, 2, 4, P], F32, name="pr", tag="pr")
+                products[(gi, m)] = pr
                 nc.vector.tensor_tensor(
                     out=pr[:],
                     in0=table[:, m].unsqueeze(2).to_broadcast([P, 2, 4, P]),
@@ -234,43 +212,72 @@ def tile_advancedattn_pa_kernel(tc, x, wq, wk, wv, out_0, out_1, out_2):
                 )
                 if ADD_ON_GPSIMD[m]:
                     rope_add(nc.gpsimd, ot, pr, m)
-                else:
-                    late.append((ot, pr, m))
             store_pair(ot, gi, 0)
-            late.append((ot, None, gi))
+
+        def rope_late_adds(gi):
+            for m in range(4):
+                if not ADD_ON_GPSIMD[m]:
+                    rope_add(nc.vector, outputs[gi], products[(gi, m)], m)
+            store_pair(outputs[gi], gi, 1)
 
         def plain_epilogue():
             for m in range(4):
                 vt = vpool.tile([P, 4, P], F32, name="vt", tag="vt")
                 accv = acc[m][:].rearrange("p (h d) -> p h d", h=4)
-                if m % 2 == 0:
+                if m < 3:
                     nc.scalar.copy(out=vt[:], in_=accv)
                 else:
                     nc.vector.tensor_copy(out=vt[:], in_=accv)
                 nc.sync.dma_start(out=out_2[0].rearrange("h (p m) d -> m p h d", m=4)[m], in_=vt[:])
 
-        def finish(gi):
-            if gi < 6:
-                rope_epilogue(gi)
-            else:
-                plain_epilogue()
-
         transpose_unit(0, 0)
+        quantize_unit(0, 0)
         transpose_unit(1, 0)
+        quantize_unit(1, 0)
         transpose_unit(0, 1)
+        quantize_unit(0, 1)
         make_tables()
         matmul_unit(1, 0)
         transpose_unit(1, 1)
+        quantize_unit(1, 1)
         transpose_unit(2, 0)
+        quantize_unit(2, 0)
         matmul_unit(1, 1)
-        finish(1)
-        for gi in range(2, N_GROUPS):
-            transpose_unit(gi, 1)
-            if gi + 1 < N_GROUPS:
-                sort_unit(gi + 1, 0)
+        rope_products(1)
+        transpose_unit(2, 1)
+        quantize_unit(2, 1)
+        rope_late_adds(1)
+        sort_unit(3, 0)
+        sort_unit(3, 1)
+        matmul_unit(2, 0)
+        transpose_unit(3, 0)
+        load(5, 0)
+        quantize_unit(3, 0)
+        transpose_unit(3, 1)
+        load(5, 1)
+        matmul_unit(2, 1)
+        rope_products(2)
+        quantize_unit(3, 1)
+        rope_late_adds(2)
+        for gi in range(3, N_GROUPS - 1):
+            nxt = gi + 1
+            sort_unit(nxt, 0)
+            transpose_unit(nxt, 0)
+            if nxt + 2 < N_GROUPS:
+                load(nxt + 2, 0)
+            quantize_unit(nxt, 0)
+            sort_unit(nxt, 1)
             matmul_unit(gi, 0)
-            if gi + 1 < N_GROUPS:
-                transpose_unit(gi + 1, 0)
-                sort_unit(gi + 1, 1)
+            transpose_unit(nxt, 1)
+            if nxt + 2 < N_GROUPS:
+                load(nxt + 2, 1)
             matmul_unit(gi, 1)
-            finish(gi)
+            if nxt == N_GROUPS - 1:
+                quantize_unit(nxt, 1)
+            rope_products(gi)
+            if nxt < N_GROUPS - 1:
+                quantize_unit(nxt, 1)
+            rope_late_adds(gi)
+        matmul_unit(N_GROUPS - 1, 0)
+        matmul_unit(N_GROUPS - 1, 1)
+        plain_epilogue()

@@ -22,7 +22,10 @@ N_GROUPS = 7
 FINE_GROUPS = 3
 ADD_ON_GPSIMD = (True, True, False, False)
 SORT_FROM_GROUP = 3
-SORTED_ROW_TILES = (1, 2, 3)
+SORTED_ROW_TILES = ((2, 3), (2, 3))
+VECTOR_COPIES = ((), ())
+HEAD_VECTOR_COPIES = ()
+HEAD_UNITS = 5
 REUSE_FROM_GROUP = 5
 
 
@@ -37,7 +40,7 @@ def tile_advancedattn_pa_kernel(tc, x, wq, wk, wv, out_0, out_1, out_2):
         epool = ctx.enter_context(tc.tile_pool(name="epool", bufs=4))
         opool = ctx.enter_context(tc.tile_pool(name="opool", bufs=3))
         vpool = ctx.enter_context(tc.tile_pool(name="vpool", bufs=4))
-        dpool = ctx.enter_context(tc.tile_pool(name="dpool", bufs=6))
+        dpool = ctx.enter_context(tc.tile_pool(name="dpool", bufs=12))
         psum = ctx.enter_context(tc.psum_pool(name="psum", bufs=1))
         ctx.enter_context(tc.manual_schedule())
 
@@ -128,21 +131,30 @@ def tile_advancedattn_pa_kernel(tc, x, wq, wk, wv, out_0, out_1, out_2):
         scales = {}
         acc = {}
         sorted_words = {}
+        sort_order = {}
         products = {}
         outputs = {}
 
-        def sort_unit(gi, a):
-            for r in SORTED_ROW_TILES:
+        def sort_unit(gi, a, tiles, eng):
+            for r in tiles:
                 dt = dpool.tile([P, 2, 2, P], F32, name="dt", tag="dt")
-                nc.scalar.copy(out=dt[:], in_=raw[(gi, a, r)].bitcast(F32).rearrange("p (g w u) -> p g u w", g=2, u=2))
+                src = raw[(gi, a, r)].bitcast(F32).rearrange("p (g w u) -> p g u w", g=2, u=2)
+                if eng == "s":
+                    nc.scalar.copy(out=dt[:], in_=src)
+                else:
+                    nc.vector.tensor_copy(out=dt[:], in_=src)
                 sorted_words[(gi, a, r)] = dt
+                sort_order.setdefault((gi, a), []).append(r)
 
-        def transpose_unit(gi, a):
+        def transpose_unit(gi, a, engines="ssss", first="u"):
             gq = gpool.tile([P, 4096], BF16, name="gq", tag="gq", align_bytes=64)
             grouped[(gi, a)] = gq
+            done = sort_order.get((gi, a), [])
+            rest = [r for r in range(4) if r not in done]
+            order = rest + done if first == "u" else done + rest
             gq_words = gq[:].bitcast(F32).rearrange("p (g r c u) -> p g r c u", g=2, r=4, u=2)
-            for r in range(4):
-                tp = psum.tile([P, 2, 2, P], F32, name="tp%d" % r, tag="tp%d" % r)
+            for pos, r in enumerate(order):
+                tp = psum.tile([P, 2, 2, P], F32, name="tp%d" % pos, tag="tp%d" % pos)
                 key = (gi, a, r)
                 for gl in range(2):
                     for u in range(2):
@@ -151,7 +163,10 @@ def tile_advancedattn_pa_kernel(tc, x, wq, wk, wv, out_0, out_1, out_2):
                         else:
                             words = raw[key].bitcast(F32)[:, 256 * gl + u : 256 * (gl + 1) : 2]
                         nc.tensor.transpose(tp[:, gl, u, :], words, ident[:])
-                nc.scalar.copy(out=gq_words[:, :, r], in_=tp[:].rearrange("p g u c -> p g c u"))
+                if engines[pos] == "v":
+                    nc.vector.tensor_copy(out=gq_words[:, :, r], in_=tp[:].rearrange("p g u c -> p g c u"))
+                else:
+                    nc.scalar.copy(out=gq_words[:, :, r], in_=tp[:].rearrange("p g u c -> p g c u"))
 
         def quantize_unit(gi, a):
             if gi == 0:
@@ -181,6 +196,23 @@ def tile_advancedattn_pa_kernel(tc, x, wq, wk, wv, out_0, out_1, out_2):
                         start=(a == 0 and gl == 0),
                         stop=(a == 1 and gl == 1),
                     )
+
+        def matmul_group(gi):
+            for m in range(4):
+                acc[m] = psum.tile([P, 512], F32, name="acc%d" % m, tag="tp%d" % m)
+                for a in range(2):
+                    for gl in range(2):
+                        tok = slice(512 * gl + P * m, 512 * gl + P * (m + 1))
+                        chan = slice(512 * gl, 512 * (gl + 1))
+                        nc.tensor.matmul_mx(
+                            out=acc[m][:],
+                            lhsT=codes[(0, a)][:, tok].bitcast(E5X4),
+                            lhsT_scale=scales[(0, a)][:, tok],
+                            rhs=codes[(gi, a)][:, chan].bitcast(E5X4),
+                            rhs_scale=scales[(gi, a)][:, chan],
+                            start=(a == 0 and gl == 0),
+                            stop=(a == 1 and gl == 1),
+                        )
 
         def rope_add(eng, ot, pr, m):
             eng.tensor_tensor(out=ot[:, :, m, 0:HALF], in0=pr[:, 0, :, 0:HALF], in1=pr[:, 1, :, HALF:P], op=ALU.add)
@@ -224,11 +256,8 @@ def tile_advancedattn_pa_kernel(tc, x, wq, wk, wv, out_0, out_1, out_2):
             for m in range(4):
                 vt = vpool.tile([P, 4, P], F32, name="vt", tag="vt")
                 accv = acc[m][:].rearrange("p (h d) -> p h d", h=4)
-                if m < 3:
-                    nc.scalar.copy(out=vt[:], in_=accv)
-                else:
-                    nc.vector.tensor_copy(out=vt[:], in_=accv)
-                nc.sync.dma_start(out=out_2[0].rearrange("h (p m) d -> m p h d", m=4)[m], in_=vt[:])
+                nc.scalar.copy(out=vt[:], in_=accv)
+                nc.scalar.dma_start(out=out_2[0].rearrange("h (p m) d -> m p h d", m=4)[m], in_=vt[:])
 
         transpose_unit(0, 0)
         quantize_unit(0, 0)
@@ -247,8 +276,8 @@ def tile_advancedattn_pa_kernel(tc, x, wq, wk, wv, out_0, out_1, out_2):
         transpose_unit(2, 1)
         quantize_unit(2, 1)
         rope_late_adds(1)
-        sort_unit(3, 0)
-        sort_unit(3, 1)
+        sort_unit(3, 0, (2, 3,), "s")
+        sort_unit(3, 1, (2, 3,), "s")
         matmul_unit(2, 0)
         transpose_unit(3, 0)
         load(5, 0)
@@ -259,25 +288,37 @@ def tile_advancedattn_pa_kernel(tc, x, wq, wk, wv, out_0, out_1, out_2):
         rope_products(2)
         quantize_unit(3, 1)
         rope_late_adds(2)
-        for gi in range(3, N_GROUPS - 1):
-            nxt = gi + 1
-            sort_unit(nxt, 0)
-            transpose_unit(nxt, 0)
-            if nxt + 2 < N_GROUPS:
-                load(nxt + 2, 0)
-            quantize_unit(nxt, 0)
-            sort_unit(nxt, 1)
-            matmul_unit(gi, 0)
-            transpose_unit(nxt, 1)
-            if nxt + 2 < N_GROUPS:
-                load(nxt + 2, 1)
-            matmul_unit(gi, 1)
-            if nxt == N_GROUPS - 1:
-                quantize_unit(nxt, 1)
-            rope_products(gi)
-            if nxt < N_GROUPS - 1:
-                quantize_unit(nxt, 1)
-            rope_late_adds(gi)
-        matmul_unit(N_GROUPS - 1, 0)
-        matmul_unit(N_GROUPS - 1, 1)
+        sort_unit(4, 0, (2, 3,), "s")
+        transpose_unit(4, 0)
+        load(6, 0)
+        quantize_unit(4, 0)
+        sort_unit(4, 1, (2, 3,), "s")
+        matmul_unit(3, 0)
+        transpose_unit(4, 1)
+        load(6, 1)
+        matmul_unit(3, 1)
+        rope_products(3)
+        quantize_unit(4, 1)
+        rope_late_adds(3)
+        sort_unit(5, 0, (2, 3,), "s")
+        transpose_unit(5, 0)
+        quantize_unit(5, 0)
+        sort_unit(5, 1, (2, 3,), "s")
+        matmul_unit(4, 0)
+        transpose_unit(5, 1)
+        matmul_unit(4, 1)
+        rope_products(4)
+        quantize_unit(5, 1)
+        rope_late_adds(4)
+        sort_unit(6, 0, (2, 3,), "s")
+        transpose_unit(6, 0)
+        quantize_unit(6, 0)
+        sort_unit(6, 1, (2, 3,), "s")
+        matmul_unit(5, 0)
+        transpose_unit(6, 1)
+        matmul_unit(5, 1)
+        quantize_unit(6, 1)
+        rope_products(5)
+        rope_late_adds(5)
+        matmul_group(6)
         plain_epilogue()

@@ -26,6 +26,7 @@ SORTED_ROW_TILES = ((2, 3), (2, 3))
 VECTOR_COPIES = ((), ())
 HEAD_VECTOR_COPIES = ()
 HEAD_UNITS = 5
+STORE_AFTER_PRODUCTS = True
 REUSE_FROM_GROUP = 5
 
 
@@ -146,14 +147,18 @@ def tile_advancedattn_pa_kernel(tc, x, wq, wk, wv, out_0, out_1, out_2):
                 sorted_words[(gi, a, r)] = dt
                 sort_order.setdefault((gi, a), []).append(r)
 
-        def transpose_unit(gi, a, engines="ssss", first="u"):
-            gq = gpool.tile([P, 4096], BF16, name="gq", tag="gq", align_bytes=64)
-            grouped[(gi, a)] = gq
+        def transpose_unit(gi, a, engines="ssss", first="u", places=(0, 1, 2, 3)):
+            if (gi, a) not in grouped:
+                gq_new = gpool.tile([P, 4096], BF16, name="gq", tag="gq", align_bytes=64)
+                grouped[(gi, a)] = gq_new
+            gq = grouped[(gi, a)]
             done = sort_order.get((gi, a), [])
             rest = [r for r in range(4) if r not in done]
             order = rest + done if first == "u" else done + rest
             gq_words = gq[:].bitcast(F32).rearrange("p (g r c u) -> p g r c u", g=2, r=4, u=2)
             for pos, r in enumerate(order):
+                if pos not in places:
+                    continue
                 tp = psum.tile([P, 2, 2, P], F32, name="tp%d" % pos, tag="tp%d" % pos)
                 key = (gi, a, r)
                 for gl in range(2):
@@ -179,9 +184,9 @@ def tile_advancedattn_pa_kernel(tc, x, wq, wk, wv, out_0, out_1, out_2):
             codes[(gi, a)] = cd
             scales[(gi, a)] = sc
 
-        def matmul_unit(gi, a):
+        def matmul_unit(gi, a, banks=(0, 1, 2, 3)):
             bank_tag = "tp%d" if gi == N_GROUPS - 1 else "acc%d"
-            for m in range(4):
+            for m in banks:
                 if a == 0:
                     acc[m] = psum.tile([P, 512], F32, name="acc%d" % m, tag=bank_tag % m)
                 for gl in range(2):
@@ -197,9 +202,10 @@ def tile_advancedattn_pa_kernel(tc, x, wq, wk, wv, out_0, out_1, out_2):
                         stop=(a == 1 and gl == 1),
                     )
 
-        def matmul_group(gi):
-            for m in range(4):
-                acc[m] = psum.tile([P, 512], F32, name="acc%d" % m, tag="tp%d" % m)
+        def matmul_group(gi, banks=(0, 1, 2, 3)):
+            bank_tag = "tp%d" if gi == N_GROUPS - 1 else "acc%d"
+            for m in banks:
+                acc[m] = psum.tile([P, 512], F32, name="acc%d" % m, tag=bank_tag % m)
                 for a in range(2):
                     for gl in range(2):
                         tok = slice(512 * gl + P * m, 512 * gl + P * (m + 1))
@@ -215,8 +221,12 @@ def tile_advancedattn_pa_kernel(tc, x, wq, wk, wv, out_0, out_1, out_2):
                         )
 
         def rope_add(eng, ot, pr, m):
-            eng.tensor_tensor(out=ot[:, :, m, 0:HALF], in0=pr[:, 0, :, 0:HALF], in1=pr[:, 1, :, HALF:P], op=ALU.add)
-            eng.tensor_tensor(out=ot[:, :, m, HALF:P], in0=pr[:, 0, :, HALF:P], in1=pr[:, 1, :, 0:HALF], op=ALU.add)
+            eng.tensor_tensor(
+                out=ot[:, :, m, :].rearrange("p h (b j) -> p h b j", b=2),
+                in0=pr[:, 0].rearrange("p h (b j) -> p h b j", b=2),
+                in1=pr[:, 1].rearrange("p h (b j) -> p h b j", b=2)[:, :, ::-1, :],
+                op=ALU.add,
+            )
 
         def store_pair(ot, gi, pair):
             if gi <= 4:
@@ -229,10 +239,12 @@ def tile_advancedattn_pa_kernel(tc, x, wq, wk, wv, out_0, out_1, out_2):
                 in_=ot[:].rearrange("p h m d -> p h (m d)")[:, :, cols],
             )
 
-        def rope_products(gi):
-            ot = opool.tile([P, 4, 4, P], F32, name="ot", tag="ot")
-            outputs[gi] = ot
-            for m in range(4):
+        def rope_products(gi, banks=(0, 1, 2, 3)):
+            if gi not in outputs:
+                ot_new = opool.tile([P, 4, 4, P], F32, name="ot", tag="ot")
+                outputs[gi] = ot_new
+            ot = outputs[gi]
+            for m in banks:
                 accv = acc[m][:].rearrange("p (h d) -> p h d", h=4)
                 pr = epool.tile([P, 2, 4, P], F32, name="pr", tag="pr")
                 products[(gi, m)] = pr
@@ -244,13 +256,14 @@ def tile_advancedattn_pa_kernel(tc, x, wq, wk, wv, out_0, out_1, out_2):
                 )
                 if ADD_ON_GPSIMD[m]:
                     rope_add(nc.gpsimd, ot, pr, m)
-            store_pair(ot, gi, 0)
+            if STORE_AFTER_PRODUCTS and 1 in banks:
+                store_pair(ot, gi, 0)
 
-        def rope_late_adds(gi):
-            for m in range(4):
+        def rope_late_adds(gi, banks=(0, 1, 2, 3)):
+            for m in banks:
                 if not ADD_ON_GPSIMD[m]:
                     rope_add(nc.vector, outputs[gi], products[(gi, m)], m)
-            store_pair(outputs[gi], gi, 1)
+            store_pair(outputs[gi], gi, banks[-1] // 2)
 
         def plain_epilogue():
             for m in range(4):
@@ -266,59 +279,91 @@ def tile_advancedattn_pa_kernel(tc, x, wq, wk, wv, out_0, out_1, out_2):
         transpose_unit(0, 1)
         quantize_unit(0, 1)
         make_tables()
-        matmul_unit(1, 0)
-        transpose_unit(1, 1)
+        matmul_unit(1, 0, (0,))
+        transpose_unit(1, 1, "ssss", "u", (0, 1,))
+        matmul_unit(1, 0, (1,))
+        transpose_unit(1, 1, "ssss", "u", (2, 3,))
         quantize_unit(1, 1)
-        transpose_unit(2, 0)
+        matmul_unit(1, 0, (2,))
+        transpose_unit(2, 0, "ssss", "u", (0, 1,))
+        matmul_unit(1, 0, (3,))
+        transpose_unit(2, 0, "ssss", "u", (2, 3,))
         quantize_unit(2, 0)
-        matmul_unit(1, 1)
-        rope_products(1)
-        transpose_unit(2, 1)
+        matmul_unit(1, 1, (0,))
+        rope_products(1, (0,))
+        transpose_unit(2, 1, "ssss", "u", (0, 1,))
+        matmul_unit(1, 1, (1,))
+        rope_products(1, (1,))
+        transpose_unit(2, 1, "ssss", "u", (2, 3,))
         quantize_unit(2, 1)
-        rope_late_adds(1)
+        matmul_unit(1, 1, (2,))
+        rope_products(1, (2,))
         sort_unit(3, 0, (2, 3,), "s")
-        sort_unit(3, 1, (2, 3,), "s")
-        matmul_unit(2, 0)
-        transpose_unit(3, 0)
+        transpose_unit(3, 0, "ssss", "u", (0, 1,))
+        matmul_unit(1, 1, (3,))
+        rope_products(1, (3,))
+        transpose_unit(3, 0, "ssss", "u", (2, 3,))
         load(5, 0)
         quantize_unit(3, 0)
-        transpose_unit(3, 1)
+        rope_late_adds(1)
+        matmul_unit(2, 0, (0, 1,))
+        sort_unit(3, 1, (2, 3,), "s")
+        transpose_unit(3, 1, "ssss", "u", (0, 1,))
+        matmul_unit(2, 0, (2, 3,))
+        transpose_unit(3, 1, "ssss", "u", (2, 3,))
         load(5, 1)
-        matmul_unit(2, 1)
-        rope_products(2)
         quantize_unit(3, 1)
-        rope_late_adds(2)
+        matmul_unit(2, 1, (0, 1,))
+        rope_products(2, (0, 1,))
         sort_unit(4, 0, (2, 3,), "s")
-        transpose_unit(4, 0)
+        transpose_unit(4, 0, "ssss", "u", (0, 1,))
+        matmul_unit(2, 1, (2, 3,))
+        rope_products(2, (2, 3,))
+        transpose_unit(4, 0, "ssss", "u", (2, 3,))
         load(6, 0)
         quantize_unit(4, 0)
+        rope_late_adds(2)
+        matmul_unit(3, 0, (0, 1,))
         sort_unit(4, 1, (2, 3,), "s")
-        matmul_unit(3, 0)
-        transpose_unit(4, 1)
+        transpose_unit(4, 1, "ssss", "u", (0, 1,))
+        matmul_unit(3, 0, (2, 3,))
+        transpose_unit(4, 1, "ssss", "u", (2, 3,))
         load(6, 1)
-        matmul_unit(3, 1)
-        rope_products(3)
         quantize_unit(4, 1)
-        rope_late_adds(3)
+        matmul_unit(3, 1, (0, 1,))
+        rope_products(3, (0, 1,))
         sort_unit(5, 0, (2, 3,), "s")
-        transpose_unit(5, 0)
+        transpose_unit(5, 0, "ssss", "u", (0, 1,))
+        matmul_unit(3, 1, (2, 3,))
+        rope_products(3, (2, 3,))
+        transpose_unit(5, 0, "ssss", "u", (2, 3,))
         quantize_unit(5, 0)
+        rope_late_adds(3)
+        matmul_unit(4, 0, (0, 1,))
         sort_unit(5, 1, (2, 3,), "s")
-        matmul_unit(4, 0)
-        transpose_unit(5, 1)
-        matmul_unit(4, 1)
-        rope_products(4)
+        transpose_unit(5, 1, "ssss", "u", (0, 1,))
+        matmul_unit(4, 0, (2, 3,))
+        transpose_unit(5, 1, "ssss", "u", (2, 3,))
         quantize_unit(5, 1)
-        rope_late_adds(4)
+        matmul_unit(4, 1, (0, 1,))
+        rope_products(4, (0, 1,))
         sort_unit(6, 0, (2, 3,), "s")
-        transpose_unit(6, 0)
+        transpose_unit(6, 0, "ssss", "u", (0, 1,))
+        matmul_unit(4, 1, (2, 3,))
+        rope_products(4, (2, 3,))
+        transpose_unit(6, 0, "ssss", "u", (2, 3,))
         quantize_unit(6, 0)
+        rope_late_adds(4)
+        matmul_unit(5, 0, (0, 1,))
         sort_unit(6, 1, (2, 3,), "s")
-        matmul_unit(5, 0)
-        transpose_unit(6, 1)
-        matmul_unit(5, 1)
+        transpose_unit(6, 1, "ssss", "u", (0, 1,))
+        matmul_unit(5, 0, (2, 3,))
+        transpose_unit(6, 1, "ssss", "u", (2, 3,))
         quantize_unit(6, 1)
-        rope_products(5)
+        matmul_unit(5, 1, (0, 1,))
+        rope_products(5, (0, 1,))
+        matmul_unit(5, 1, (2, 3,))
+        rope_products(5, (2, 3,))
         rope_late_adds(5)
         matmul_group(6)
         plain_epilogue()

@@ -295,13 +295,13 @@ def tile_advancedattn_pa_kernel(tc, x, wq, wk, wv, out_0, out_1, out_2):
         matmul_unit(1, 1, (1,))
         rope_products(1, (1,))
         transpose_unit(2, 1, "ssss", "u", (2, 3,))
-        quantize_unit(2, 1)
         matmul_unit(1, 1, (2,))
         rope_products(1, (2,))
         sort_unit(3, 0, (2, 3,), "s")
         transpose_unit(3, 0, "ssss", "u", (0, 1,))
         matmul_unit(1, 1, (3,))
         rope_products(1, (3,))
+        quantize_unit(2, 1)
         transpose_unit(3, 0, "ssss", "u", (2, 3,))
         load(5, 0)
         quantize_unit(3, 0)
@@ -312,13 +312,13 @@ def tile_advancedattn_pa_kernel(tc, x, wq, wk, wv, out_0, out_1, out_2):
         matmul_unit(2, 0, (2, 3,))
         transpose_unit(3, 1, "ssss", "u", (2, 3,))
         load(5, 1)
-        quantize_unit(3, 1)
         matmul_unit(2, 1, (0, 1,))
         rope_products(2, (0, 1,))
         sort_unit(4, 0, (2, 3,), "s")
         transpose_unit(4, 0, "ssss", "u", (0, 1,))
         matmul_unit(2, 1, (2, 3,))
         rope_products(2, (2, 3,))
+        quantize_unit(3, 1)
         transpose_unit(4, 0, "ssss", "u", (2, 3,))
         load(6, 0)
         quantize_unit(4, 0)
@@ -329,13 +329,13 @@ def tile_advancedattn_pa_kernel(tc, x, wq, wk, wv, out_0, out_1, out_2):
         matmul_unit(3, 0, (2, 3,))
         transpose_unit(4, 1, "ssss", "u", (2, 3,))
         load(6, 1)
-        quantize_unit(4, 1)
         matmul_unit(3, 1, (0, 1,))
         rope_products(3, (0, 1,))
         sort_unit(5, 0, (2, 3,), "s")
         transpose_unit(5, 0, "ssss", "u", (0, 1,))
         matmul_unit(3, 1, (2, 3,))
         rope_products(3, (2, 3,))
+        quantize_unit(4, 1)
         transpose_unit(5, 0, "ssss", "u", (2, 3,))
         quantize_unit(5, 0)
         rope_late_adds(3)
@@ -344,13 +344,13 @@ def tile_advancedattn_pa_kernel(tc, x, wq, wk, wv, out_0, out_1, out_2):
         transpose_unit(5, 1, "ssss", "u", (0, 1,))
         matmul_unit(4, 0, (2, 3,))
         transpose_unit(5, 1, "ssss", "u", (2, 3,))
-        quantize_unit(5, 1)
         matmul_unit(4, 1, (0, 1,))
         rope_products(4, (0, 1,))
         sort_unit(6, 0, (2, 3,), "s")
         transpose_unit(6, 0, "ssss", "u", (0, 1,))
         matmul_unit(4, 1, (2, 3,))
         rope_products(4, (2, 3,))
+        quantize_unit(5, 1)
         transpose_unit(6, 0, "ssss", "u", (2, 3,))
         quantize_unit(6, 0)
         rope_late_adds(4)

@@ -281,9 +281,11 @@ def tile_advancedattn_pa_kernel(tc, x, wq, wk, wv, out_0, out_1, out_2):
         make_tables()
         matmul_unit(1, 0, (0,))
         transpose_unit(1, 1, "ssss", "u", (0, 1,))
+        sort_unit(2, 0, (2, 3,), "v")
         matmul_unit(1, 0, (1,))
         transpose_unit(1, 1, "ssss", "u", (2, 3,))
         quantize_unit(1, 1)
+        sort_unit(2, 1, (0, 1, 2, 3,), "v")
         matmul_unit(1, 0, (2,))
         transpose_unit(2, 0, "ssss", "u", (0, 1,))
         matmul_unit(1, 0, (3,))

from contextlib import ExitStack

import concourse.mybir as mybir
from concourse.masks import make_identity

F32 = mybir.dt.float32
BF16 = mybir.dt.bfloat16
I32 = mybir.dt.int32
U32 = mybir.dt.uint32
U8 = mybir.dt.uint8
E5X4 = mybir.dt.float8_e5m2_x4
ALU = mybir.AluOpType
ACT = mybir.ActivationFunctionType

FLOPS = 2 * 512 * 2048 * 3072

P = 128
HALF = 64
THETA = 10000.0
TWO_PI = 6.283185307179586
N_GROUPS = 7
FINE_GROUPS = 3
ADD_ON_GPSIMD = (True, True, False, False)
SORT_FROM_GROUP = 3
SORTED_ROW_TILES = ((2, 3), (2, 3))
VECTOR_COPIES = ((), ())
HEAD_VECTOR_COPIES = ()
HEAD_UNITS = 5
STORE_AFTER_PRODUCTS = True
REUSE_FROM_GROUP = 5


def tile_advancedattn_pa_kernel(tc, x, wq, wk, wv, out_0, out_1, out_2):
    nc = tc.nc

    with ExitStack() as ctx:
        const = ctx.enter_context(tc.tile_pool(name="const", bufs=1))
        rawp = ctx.enter_context(tc.tile_pool(name="rawp", bufs=1))
        gpool = ctx.enter_context(tc.tile_pool(name="gpool", bufs=3))
        cpool = ctx.enter_context(tc.tile_pool(name="cpool", bufs=4))
        epool = ctx.enter_context(tc.tile_pool(name="epool", bufs=4))
        opool = ctx.enter_context(tc.tile_pool(name="opool", bufs=3))
        vpool = ctx.enter_context(tc.tile_pool(name="vpool", bufs=4))
        dpool = ctx.enter_context(tc.tile_pool(name="dpool", bufs=12))
        psum = ctx.enter_context(tc.psum_pool(name="psum", bufs=1))
        ctx.enter_context(tc.manual_schedule())

        raw = {}

        def group_rows(gi):
            if gi <= 4:
                return wq[512 * (gi - 1) : 512 * gi, :]
            if gi == 5:
                return wk
            return wv

        def load(gi, a):
            cols = slice(1024 * a, 1024 * (a + 1))
            if gi < FINE_GROUPS:
                for r in range(4):
                    t = rawp.tile([P, 1024], BF16, name="raw%d_%d_%d" % (gi, a, r), tag="raw%d_%d_%d" % (gi, a, r))
                    if gi == 0:
                        src = x[0].rearrange("(p m) k -> m p k", m=4)[r]
                    else:
                        src = group_rows(gi)[P * r : P * (r + 1), :]
                    nc.sync.dma_start(out=t[:], in_=src[:, cols])
                    raw[(gi, a, r)] = t[:]
            else:
                slot = gi - 2 if gi >= REUSE_FROM_GROUP else gi
                t = rawp.tile([P, 4, 1024], BF16, name="raw%d_%d" % (gi, a), tag="raw%d_%d" % (slot, a))
                nc.sync.dma_start(out=t[:], in_=group_rows(gi)[:, cols].rearrange("(r p) k -> p r k", p=P))
                for r in range(4):
                    raw[(gi, a, r)] = t[:, r, :]

        for gi, a in ((0, 0), (1, 0), (0, 1), (1, 1)):
            load(gi, a)
        for gi in range(2, REUSE_FROM_GROUP):
            load(gi, 0)
            load(gi, 1)

        ident = const.tile([P, P], F32, name="ident", tag="ident")
        make_identity(nc, ident[:])
        pos_i = const.tile([P, 4], I32, name="pos_i", tag="pos_i")
        nc.gpsimd.iota(pos_i[:], pattern=[[1, 4]], base=0, channel_multiplier=4)

        zero = const.tile([P, 1], F32, name="zero", tag="zero")
        warm = const.tile([P, 1], F32, name="warm", tag="warm")
        nc.vector.memset(zero[:], 0.0)
        nc.scalar.activation(out=warm[:], in_=zero[:], func=ACT.Sin)

        freq = const.tile([P, HALF], F32, name="freq", tag="freq")
        nc.vector.memset(freq[:, 0:1], 1.0)
        s = 1
        while s < HALF:
            nc.vector.tensor_scalar(
                out=freq[:, s : 2 * s], in0=freq[:, 0:s], scalar1=THETA ** (-s / float(HALF)), scalar2=None, op0=ALU.mult
            )
            s *= 2
        pos_f = const.tile([P, 4], F32, name="pos_f", tag="pos_f")
        nc.vector.tensor_copy(out=pos_f[:], in_=pos_i[:])
        turns = const.tile([P, 4, HALF], F32, name="turns", tag="turns")
        for m in range(4):
            nc.vector.tensor_scalar(
                out=turns[:, m, :], in0=freq[:], scalar1=pos_f[:, m : m + 1], scalar2=1.0 / TWO_PI, op0=ALU.mult, op1=ALU.mult
            )
        whole_i = const.tile([P, 4, HALF], I32, name="whole_i", tag="whole_i")
        whole_f = const.tile([P, 4, HALF], F32, name="whole_f", tag="whole_f")
        nc.vector.tensor_copy(out=whole_i[:], in_=turns[:])
        nc.vector.tensor_copy(out=whole_f[:], in_=whole_i[:])
        arg = const.tile([P, 2, 4, HALF], F32, name="arg", tag="arg")
        nc.vector.tensor_tensor(out=arg[:, 0], in0=turns[:], in1=whole_f[:], op=ALU.subtract)
        nc.vector.tensor_scalar(out=arg[:, 1], in0=arg[:, 0], scalar1=0.25, scalar2=None, op0=ALU.add)
        wrap = const.tile([P, 2, 4, HALF], F32, name="wrap", tag="wrap")
        nc.vector.scalar_tensor_tensor(
            out=wrap[:].rearrange("p a m j -> p (a m j)"),
            in0=arg[:].rearrange("p a m j -> p (a m j)"),
            scalar=0.5,
            in1=arg[:].rearrange("p a m j -> p (a m j)"),
            op0=ALU.is_gt,
            op1=ALU.subtract,
        )
        table = const.tile([P, 4, 2, P], F32, name="table", tag="table")

        def make_tables():
            nc.scalar.activation(out=table[:, :, 0, 0:HALF], in_=wrap[:, 1], func=ACT.Sin, scale=-TWO_PI)
            nc.scalar.activation(out=table[:, :, 0, HALF:P], in_=wrap[:, 1], func=ACT.Sin, scale=-TWO_PI)
            nc.scalar.activation(out=table[:, :, 1, 0:HALF], in_=wrap[:, 0], func=ACT.Sin, scale=-TWO_PI)
            nc.scalar.activation(out=table[:, :, 1, HALF:P], in_=wrap[:, 0], func=ACT.Sin, scale=TWO_PI)

        grouped = {}
        codes = {}
        scales = {}
        acc = {}
        sorted_words = {}
        sort_order = {}
        products = {}
        outputs = {}

        def sort_unit(gi, a, tiles, eng):
            for r in tiles:
                dt = dpool.tile([P, 2, 2, P], F32, name="dt", tag="dt")
                src = raw[(gi, a, r)].bitcast(F32).rearrange("p (g w u) -> p g u w", g=2, u=2)
                if eng == "s":
                    nc.scalar.copy(out=dt[:], in_=src)
                else:
                    nc.vector.tensor_copy(out=dt[:], in_=src)
                sorted_words[(gi, a, r)] = dt
                sort_order.setdefault((gi, a), []).append(r)

        def transpose_unit(gi, a, engines="ssss", first="u", places=(0, 1, 2, 3)):
            if (gi, a) not in grouped:
                gq_new = gpool.tile([P, 4096], BF16, name="gq", tag="gq", align_bytes=64)
                grouped[(gi, a)] = gq_new
            gq = grouped[(gi, a)]
            done = sort_order.get((gi, a), [])
            rest = [r for r in range(4) if r not in done]
            order = rest + done if first == "u" else done + rest
            gq_words = gq[:].bitcast(F32).rearrange("p (g r c u) -> p g r c u", g=2, r=4, u=2)
            for pos, r in enumerate(order):
                if pos not in places:
                    continue
                tp = psum.tile([P, 2, 2, P], F32, name="tp%d" % pos, tag="tp%d" % pos)
                key = (gi, a, r)
                for gl in range(2):
                    for u in range(2):
                        if key in sorted_words:
                            words = sorted_words[key][:, gl, u, :]
                        else:
                            words = raw[key].bitcast(F32)[:, 256 * gl + u : 256 * (gl + 1) : 2]
                        nc.tensor.transpose(tp[:, gl, u, :], words, ident[:])
                if engines[pos] == "v":
                    nc.vector.tensor_copy(out=gq_words[:, :, r], in_=tp[:].rearrange("p g u c -> p g c u"))
                else:
                    nc.scalar.copy(out=gq_words[:, :, r], in_=tp[:].rearrange("p g u c -> p g c u"))

        def quantize_unit(gi, a):
            if gi == 0:
                cd = const.tile([P, 1024], U32, name="xc%d" % a, tag="xc%d" % a, align_bytes=64)
                sc = const.tile([P, 1024], U8, name="xs%d" % a, tag="xs%d" % a, align_bytes=64)
            else:
                cd = cpool.tile([P, 1024], U32, name="wc", tag="wc", align_bytes=64)
                sc = cpool.tile([P, 1024], U8, name="ws", tag="ws", align_bytes=64)
            nc.vector.quantize_mx(out=cd[:].bitcast(E5X4), scales=sc[:], in_=grouped[(gi, a)][:])
            codes[(gi, a)] = cd
            scales[(gi, a)] = sc

        def matmul_unit(gi, a, banks=(0, 1, 2, 3)):
            bank_tag = "tp%d" if gi == N_GROUPS - 1 else "acc%d"
            for m in banks:
                if a == 0:
                    acc[m] = psum.tile([P, 512], F32, name="acc%d" % m, tag=bank_tag % m)
                for gl in range(2):
                    tok = slice(512 * gl + P * m, 512 * gl + P * (m + 1))
                    chan = slice(512 * gl, 512 * (gl + 1))
                    nc.tensor.matmul_mx(
                        out=acc[m][:],
                        lhsT=codes[(0, a)][:, tok].bitcast(E5X4),
                        lhsT_scale=scales[(0, a)][:, tok],
                        rhs=codes[(gi, a)][:, chan].bitcast(E5X4),
                        rhs_scale=scales[(gi, a)][:, chan],
                        start=(a == 0 and gl == 0),
                        stop=(a == 1 and gl == 1),
                    )

        def matmul_group(gi, banks=(0, 1, 2, 3)):
            bank_tag = "tp%d" if gi == N_GROUPS - 1 else "acc%d"
            for m in banks:
                acc[m] = psum.tile([P, 512], F32, name="acc%d" % m, tag=bank_tag % m)
                for a in range(2):
                    for gl in range(2):
                        tok = slice(512 * gl + P * m, 512 * gl + P * (m + 1))
                        chan = slice(512 * gl, 512 * (gl + 1))
                        nc.tensor.matmul_mx(
                            out=acc[m][:],
                            lhsT=codes[(0, a)][:, tok].bitcast(E5X4),
                            lhsT_scale=scales[(0, a)][:, tok],
                            rhs=codes[(gi, a)][:, chan].bitcast(E5X4),
                            rhs_scale=scales[(gi, a)][:, chan],
                            start=(a == 0 and gl == 0),
                            stop=(a == 1 and gl == 1),
                        )

        def rope_add(eng, ot, pr, m):
            eng.tensor_tensor(
                out=ot[:, :, m, :].rearrange("p h (b j) -> p h b j", b=2),
                in0=pr[:, 0].rearrange("p h (b j) -> p h b j", b=2),
                in1=pr[:, 1].rearrange("p h (b j) -> p h b j", b=2)[:, :, ::-1, :],
                op=ALU.add,
            )

        def store_pair(ot, gi, pair):
            if gi <= 4:
                dst = out_0[0, 4 * (gi - 1) : 4 * gi]
            else:
                dst = out_1[0]
            cols = slice(2 * P * pair, 2 * P * (pair + 1))
            nc.sync.dma_start(
                out=dst.rearrange("h (p m) d -> p h (m d)", m=4)[:, :, cols],
                in_=ot[:].rearrange("p h m d -> p h (m d)")[:, :, cols],
            )

        def rope_products(gi, banks=(0, 1, 2, 3)):
            if gi not in outputs:
                ot_new = opool.tile([P, 4, 4, P], F32, name="ot", tag="ot")
                outputs[gi] = ot_new
            ot = outputs[gi]
            for m in banks:
                accv = acc[m][:].rearrange("p (h d) -> p h d", h=4)
                pr = epool.tile([P, 2, 4, P], F32, name="pr", tag="pr")
                products[(gi, m)] = pr
                nc.vector.tensor_tensor(
                    out=pr[:],
                    in0=table[:, m].unsqueeze(2).to_broadcast([P, 2, 4, P]),
                    in1=accv.unsqueeze(1).to_broadcast([P, 2, 4, P]),
                    op=ALU.mult,
                )
                if ADD_ON_GPSIMD[m]:
                    rope_add(nc.gpsimd, ot, pr, m)
            if STORE_AFTER_PRODUCTS and 1 in banks:
                store_pair(ot, gi, 0)

        def rope_late_adds(gi, banks=(0, 1, 2, 3)):
            for m in banks:
                if not ADD_ON_GPSIMD[m]:
                    rope_add(nc.vector, outputs[gi], products[(gi, m)], m)
            store_pair(outputs[gi], gi, banks[-1] // 2)

        def plain_epilogue():
            for m in range(4):
                vt = vpool.tile([P, 4, P], F32, name="vt", tag="vt")
                accv = acc[m][:].rearrange("p (h d) -> p h d", h=4)
                nc.scalar.copy(out=vt[:], in_=accv)
                nc.scalar.dma_start(out=out_2[0].rearrange("h (p m) d -> m p h d", m=4)[m], in_=vt[:])

        transpose_unit(0, 0)
        quantize_unit(0, 0)
        transpose_unit(1, 0)
        quantize_unit(1, 0)
        transpose_unit(0, 1)
        quantize_unit(0, 1)
        make_tables()
        matmul_unit(1, 0, (0,))
        transpose_unit(1, 1, "ssss", "u", (0, 1,))
        sort_unit(2, 0, (2, 3,), "v")
        matmul_unit(1, 0, (1,))
        transpose_unit(1, 1, "ssss", "u", (2, 3,))
        quantize_unit(1, 1)
        sort_unit(2, 1, (0, 1, 2, 3,), "v")
        matmul_unit(1, 0, (2,))
        transpose_unit(2, 0, "ssss", "u", (0, 1,))
        matmul_unit(1, 0, (3,))
        transpose_unit(2, 0, "ssss", "u", (2, 3,))
        quantize_unit(2, 0)
        matmul_unit(1, 1, (0,))
        rope_products(1, (0,))
        transpose_unit(2, 1, "ssss", "u", (0, 1,))
        matmul_unit(1, 1, (1,))
        rope_products(1, (1,))
        transpose_unit(2, 1, "ssss", "u", (2, 3,))
        matmul_unit(1, 1, (2,))
        rope_products(1, (2,))
        sort_unit(3, 0, (2, 3,), "s")
        transpose_unit(3, 0, "ssss", "u", (0, 1,))
        matmul_unit(1, 1, (3,))
        rope_products(1, (3,))
        quantize_unit(2, 1)
        transpose_unit(3, 0, "ssss", "u", (2, 3,))
        load(5, 0)
        quantize_unit(3, 0)
        rope_late_adds(1)
        matmul_unit(2, 0, (0, 1,))
        sort_unit(3, 1, (2, 3,), "s")
        transpose_unit(3, 1, "ssss", "u", (0, 1,))
        matmul_unit(2, 0, (2, 3,))
        transpose_unit(3, 1, "ssss", "u", (2, 3,))
        load(5, 1)
        matmul_unit(2, 1, (0, 1,))
        rope_products(2, (0, 1,))
        sort_unit(4, 0, (2, 3,), "s")
        transpose_unit(4, 0, "ssss", "u", (0, 1,))
        matmul_unit(2, 1, (2, 3,))
        rope_products(2, (2, 3,))
        quantize_unit(3, 1)
        transpose_unit(4, 0, "ssss", "u", (2, 3,))
        load(6, 0)
        quantize_unit(4, 0)
        rope_late_adds(2)
        matmul_unit(3, 0, (0, 1,))
        sort_unit(4, 1, (2, 3,), "s")
        transpose_unit(4, 1, "ssss", "u", (0, 1,))
        matmul_unit(3, 0, (2, 3,))
        transpose_unit(4, 1, "ssss", "u", (2, 3,))
        load(6, 1)
        matmul_unit(3, 1, (0, 1,))
        rope_products(3, (0, 1,))
        sort_unit(5, 0, (2, 3,), "s")
        transpose_unit(5, 0, "ssss", "u", (0, 1,))
        matmul_unit(3, 1, (2, 3,))
        rope_products(3, (2, 3,))
        quantize_unit(4, 1)
        transpose_unit(5, 0, "ssss", "u", (2, 3,))
        quantize_unit(5, 0)
        rope_late_adds(3)
        matmul_unit(4, 0, (0, 1,))
        sort_unit(5, 1, (2, 3,), "s")
        transpose_unit(5, 1, "ssss", "u", (0, 1,))
        matmul_unit(4, 0, (2, 3,))
        transpose_unit(5, 1, "ssss", "u", (2, 3,))
        matmul_unit(4, 1, (0, 1,))
        rope_products(4, (0, 1,))
        sort_unit(6, 0, (2, 3,), "s")
        transpose_unit(6, 0, "ssss", "u", (0, 1,))
        matmul_unit(4, 1, (2, 3,))
        rope_products(4, (2, 3,))
        quantize_unit(5, 1)
        transpose_unit(6, 0, "ssss", "u", (2, 3,))
        quantize_unit(6, 0)
        rope_late_adds(4)
        matmul_unit(5, 0, (0, 1,))
        sort_unit(6, 1, (2, 3,), "s")
        transpose_unit(6, 1, "ssss", "u", (0, 1,))
        matmul_unit(5, 0, (2, 3,))
        transpose_unit(6, 1, "ssss", "u", (2, 3,))
        quantize_unit(6, 1)
        matmul_unit(5, 1, (0, 1,))
        rope_products(5, (0, 1,))
        matmul_unit(5, 1, (2, 3,))
        rope_products(5, (2, 3,))
        rope_late_adds(5)
        matmul_group(6)
        plain_epilogue()
